import numpy as np
import ml_dtypes


def mxq(x, axis, fmt="e4m3"):
    dtype, down = {"e4m3": (ml_dtypes.float8_e4m3fn, 7), "e5m2": (ml_dtypes.float8_e5m2, 14)}[fmt]
    v = np.moveaxis(np.asarray(x, np.float32).astype(ml_dtypes.bfloat16).astype(np.float64), axis, -1)
    blocks = v.reshape(v.shape[:-1] + (-1, 32))
    amax = np.abs(blocks).max(-1, keepdims=True)
    byte = np.maximum(np.where(amax > 0, np.frexp(amax)[1] - 1 + 127, 0) - down, 1)
    scale = np.exp2(byte - 127.0)
    codes = (blocks / scale).astype(np.float32).astype(dtype).astype(np.float64)
    return np.moveaxis((codes * scale).reshape(v.shape), -1, axis)


WIDE = False


def mx_kscale(k):
    if not WIDE:
        return np.ones(k)
    levels = np.array([20, -20, 10, -10, 0])
    a = np.random.permutation(np.resize(levels, k // 512 * 4)).reshape(k // 512, 4)
    idx = np.arange(k)
    return np.exp2(a[idx // 512, idx % 128 // 32])


BF16 = ml_dtypes.bfloat16


def bf(x):
    return np.asarray(x, np.float32).astype(BF16)


def f64(x):
    return np.asarray(x).astype(np.float64)


B, IN, OUT, R, Q, ORD = 1024, 1024, 1024, 8, 512, 3
K = R ** ORD


def kron_of(Z):
    kron = Z[0]
    for j in range(1, ORD):
        kron = kron[None] * Z[j].reshape((R,) + (1,) * j + (B,))
    return kron.reshape((-1, B))


def setup_inputs():
    s = mx_kscale(B)
    z = np.random.standard_normal((ORD, R, B))
    z[ORD - 1] *= s[None, :]
    g = np.random.standard_normal((Q, K)) / np.sqrt(K)
    go = np.random.standard_normal((Q, B)) * np.exp2(np.random.randint(-12, 1, (1, B))) * 0.25 / s[None, :]
    return {"z": bf(z), "G2": bf(g), "grad_out": bf(go)}


def reference(z, G2, grad_out):
    kron = kron_of(f64(z))
    return mxq(f64(grad_out), 1, "e5m2") @ mxq(kron, 1, "e4m3").T

@@ -1,0 +1,136 @@
+from contextlib import ExitStack
+
+import concourse.mybir as mybir
+from concourse.masks import make_identity
+
+F32 = mybir.dt.float32
+BF16 = mybir.dt.bfloat16
+U32 = mybir.dt.uint32
+U8 = mybir.dt.uint8
+E4M3_X4 = mybir.dt.float8_e4m3fn_x4
+E5M2_X4 = mybir.dt.float8_e5m2_x4
+MULT = mybir.AluOpType.mult
+
+P = 128
+PACK = 4
+PAIR = 2
+HALVES = PACK // PAIR
+K_PASS = P * PACK
+
+ORD, R, B = 3, 8, 1024
+Q = 512
+K = R**ORD
+PASSES = B // K_PASS
+Q_TILES = Q // P
+CHUNKS = PASSES * HALVES
+
+FLOPS = 2 * Q * K * B
+BYTES = ORD * R * B * 2 + Q * B * 2 + Q * K * 4
+
+
+def tile_fast_tucker_taylor_pa_s_kernel(tc, z, G2, grad_out, out):
+    nc = tc.nc
+    with ExitStack() as stack:
+        consts = stack.enter_context(tc.tile_pool(name="consts", bufs=1))
+        factors = stack.enter_context(tc.tile_pool(name="factors", bufs=1))
+        per_pass = stack.enter_context(tc.tile_pool(name="per_pass", bufs=PASSES))
+        operands = stack.enter_context(tc.tile_pool(name="operands", bufs=1))
+        results = stack.enter_context(tc.tile_pool(name="results", bufs=Q_TILES))
+        psum_z = stack.enter_context(tc.psum_pool(name="psum_z", bufs=1))
+        psum_t = stack.enter_context(tc.psum_pool(name="psum_t", bufs=3))
+        psum_acc = stack.enter_context(tc.psum_pool(name="psum_acc", bufs=1))
+
+        z_rows = factors.tile([P, P * PAIR], BF16)
+        live = ORD * R * CHUNKS
+        nc.vector.memset(z_rows[live:P, :], 0.0)
+        nc.sync.dma_start(out=z_rows[0:live, :], in_=z.rearrange("j r (h w) -> (j r h) w", h=CHUNKS))
+
+        grad_rows = []
+        for g in range(PASSES):
+            rows = per_pass.tile([P, Q_TILES, K_PASS], BF16, name="grad_rows")
+            nc.sync.dma_start(
+                out=rows[:],
+                in_=grad_out[:, g * K_PASS : (g + 1) * K_PASS].rearrange("(i p) n -> p i n", p=P),
+            )
+            grad_rows.append(rows)
+
+        identity = consts.tile([P, P], F32)
+        make_identity(nc, identity[:])
+
+        z_cols = psum_z.tile([P, P], F32)
+        nc.tensor.transpose(z_cols[:], z_rows[:].bitcast(F32), identity[:])
+        z_f32 = factors.tile([P, ORD * R, PASSES * PACK], F32)
+        nc.vector.tensor_copy(
+            out=z_f32[:].rearrange("p r i -> p (r i)"), in_=z_cols[:, 0:live].bitcast(BF16)
+        )
+
+        grad_grouped = []
+        for g in range(PASSES):
+            grouped = per_pass.tile([P, Q_TILES * P * PACK], BF16, name="grad_grouped", align_bytes=64)
+            grouped_words = grouped[:].bitcast(F32).rearrange(
+                "p (i q u) -> p i q u", i=Q_TILES, u=HALVES
+            )
+            for first in range(0, Q_TILES, 2):
+                bank = psum_t.tile([P, 2, HALVES, P], F32, name="bank")
+                for i in range(2):
+                    words = grad_rows[g][:, first + i, :].bitcast(F32)
+                    for u in range(HALVES):
+                        nc.tensor.transpose(bank[:, i, u, :], words[:, u * P : (u + 1) * P], identity[:])
+                nc.scalar.copy(
+                    out=grouped_words[:, first : first + 2],
+                    in_=bank[:].rearrange("p i u q -> p i q u"),
+                )
+            grad_grouped.append(grouped)
+
+        kron_codes = operands.tile([P, PASSES, K], U32, align_bytes=64)
+        kron_scales = operands.tile([P, PASSES, K], U8, align_bytes=64)
+        grad_codes = operands.tile([P, PASSES, Q], U32, align_bytes=64)
+        grad_scales = operands.tile([P, PASSES, Q], U8, align_bytes=64)
+        acc = [psum_acc.tile([P, K], F32, name="acc%d" % i) for i in range(Q_TILES)]
+
+        pair01 = factors.tile([P, R, R, PASSES * PACK], F32)
+        nc.vector.tensor_tensor(
+            out=pair01[:],
+            in0=z_f32[:, 0:R, :].unsqueeze(1).to_broadcast([P, R, R, PASSES * PACK]),
+            in1=z_f32[:, R : 2 * R, :].unsqueeze(2).to_broadcast([P, R, R, PASSES * PACK]),
+            op=MULT,
+        )
+
+        for g in range(PASSES):
+            t_cols = slice(g * PACK, (g + 1) * PACK)
+            kron = per_pass.tile([P, R, R * R, PACK], BF16, name="kron", align_bytes=64)
+            nc.vector.tensor_tensor(
+                out=kron[:],
+                in0=pair01[:, :, :, t_cols].rearrange("p b a t -> p (b a) t").unsqueeze(1).to_broadcast([P, R, R * R, PACK]),
+                in1=z_f32[:, 2 * R : 3 * R, t_cols].unsqueeze(2).to_broadcast([P, R, R * R, PACK]),
+                op=MULT,
+            )
+            nc.vector.quantize_mx(
+                out=grad_codes[:, g, :].bitcast(E5M2_X4),
+                scales=grad_scales[:, g, :],
+                in_=grad_grouped[g][:],
+            )
+            nc.vector.quantize_mx(
+                out=kron_codes[:, g, :].bitcast(E4M3_X4),
+                scales=kron_scales[:, g, :],
+                in_=kron[:].rearrange("p c w t -> p (c w t)"),
+            )
+            for i in range(Q_TILES):
+                q_cols = slice(i * P, (i + 1) * P)
+                nc.tensor.matmul_mx(
+                    out=acc[i][:],
+                    lhsT=grad_codes[:, g, q_cols].bitcast(E5M2_X4),
+                    lhsT_scale=grad_scales[:, g, q_cols],
+                    rhs=kron_codes[:, g, :].bitcast(E4M3_X4),
+                    rhs_scale=kron_scales[:, g, :],
+                    start=(g == 0),
+                    stop=(g == PASSES - 1),
+                )
+
+        for i in range(Q_TILES):
+            result = results.tile([P, K], F32, name="result")
+            if i % 2 == 0:
+                nc.scalar.copy(out=result[:], in_=acc[i][:])
+            else:
+                nc.vector.tensor_copy(out=result[:], in_=acc[i][:])
+            nc.sync.dma_start(out=out[i * P : (i + 1) * P, :], in_=result[:])

@@ -40,10 +40,12 @@ def tile_fast_tucker_taylor_pa_s_kernel(tc, z, G2, grad_out, out):
         psum_t = stack.enter_context(tc.psum_pool(name="psum_t", bufs=3))
         psum_acc = stack.enter_context(tc.psum_pool(name="psum_acc", bufs=1))
 
+        z_runs = z.rearrange("j r (h w) -> (j r h) w", h=CHUNKS)
+        runs_of_two = 2 * R * CHUNKS
+        runs_of_one = R * CHUNKS
         z_rows = factors.tile([P, P * PAIR], BF16)
-        live = ORD * R * CHUNKS
-        nc.vector.memset(z_rows[live:P, :], 0.0)
-        nc.sync.dma_start(out=z_rows[0:live, :], in_=z.rearrange("j r (h w) -> (j r h) w", h=CHUNKS))
+        nc.sync.dma_start(out=z_rows[0:runs_of_two, :], in_=z_runs[0:runs_of_two, :])
+        nc.sync.dma_start(out=z_rows[runs_of_two:P, :], in_=z_runs[runs_of_one : runs_of_one + runs_of_two, :])
 
         grad_rows = []
         for g in range(PASSES):
@@ -59,10 +61,11 @@ def tile_fast_tucker_taylor_pa_s_kernel(tc, z, G2, grad_out, out):
 
         z_cols = psum_z.tile([P, P], F32)
         nc.tensor.transpose(z_cols[:], z_rows[:].bitcast(F32), identity[:])
-        z_f32 = factors.tile([P, ORD * R, PASSES * PACK], F32)
-        nc.vector.tensor_copy(
-            out=z_f32[:].rearrange("p r i -> p (r i)"), in_=z_cols[:, 0:live].bitcast(BF16)
-        )
+        z_f32 = factors.tile([P, 4 * R, PASSES * PACK], F32)
+        nc.vector.tensor_copy(out=z_f32[:].rearrange("p r i -> p (r i)"), in_=z_cols[:].bitcast(BF16))
+        z0 = z_f32[:, 0:R, :]
+        z1 = z_f32[:, R : 2 * R, :]
+        z2 = z_f32[:, 3 * R : 4 * R, :]
 
         grad_grouped = []
         for g in range(PASSES):
@@ -91,8 +94,8 @@ def tile_fast_tucker_taylor_pa_s_kernel(tc, z, G2, grad_out, out):
         pair01 = factors.tile([P, R, R, PASSES * PACK], F32)
         nc.vector.tensor_tensor(
             out=pair01[:],
-            in0=z_f32[:, 0:R, :].unsqueeze(1).to_broadcast([P, R, R, PASSES * PACK]),
-            in1=z_f32[:, R : 2 * R, :].unsqueeze(2).to_broadcast([P, R, R, PASSES * PACK]),
+            in0=z0.unsqueeze(1).to_broadcast([P, R, R, PASSES * PACK]),
+            in1=z1.unsqueeze(2).to_broadcast([P, R, R, PASSES * PACK]),
             op=MULT,
         )
 
@@ -102,7 +105,7 @@ def tile_fast_tucker_taylor_pa_s_kernel(tc, z, G2, grad_out, out):
             nc.vector.tensor_tensor(
                 out=kron[:],
                 in0=pair01[:, :, :, t_cols].rearrange("p b a t -> p (b a) t").unsqueeze(1).to_broadcast([P, R, R * R, PACK]),
-                in1=z_f32[:, 2 * R : 3 * R, t_cols].unsqueeze(2).to_broadcast([P, R, R * R, PACK]),
+                in1=z2[:, :, t_cols].unsqueeze(2).to_broadcast([P, R, R * R, PACK]),
                 op=MULT,
             )
             nc.vector.quantize_mx(

@@ -39,6 +39,7 @@ def tile_fast_tucker_taylor_pa_s_kernel(tc, z, G2, grad_out, out):
         psum_z = stack.enter_context(tc.psum_pool(name="psum_z", bufs=1))
         psum_t = stack.enter_context(tc.psum_pool(name="psum_t", bufs=3))
         psum_acc = stack.enter_context(tc.psum_pool(name="psum_acc", bufs=1))
+        stack.enter_context(tc.manual_schedule())
 
         z_runs = z.rearrange("j r (h w) -> (j r h) w", h=CHUNKS)
         runs_of_two = 2 * R * CHUNKS
@@ -85,12 +86,6 @@ def tile_fast_tucker_taylor_pa_s_kernel(tc, z, G2, grad_out, out):
                 )
             grad_grouped.append(grouped)
 
-        kron_codes = operands.tile([P, PASSES, K], U32, align_bytes=64)
-        kron_scales = operands.tile([P, PASSES, K], U8, align_bytes=64)
-        grad_codes = operands.tile([P, PASSES, Q], U32, align_bytes=64)
-        grad_scales = operands.tile([P, PASSES, Q], U8, align_bytes=64)
-        acc = [psum_acc.tile([P, K], F32, name="acc%d" % i) for i in range(Q_TILES)]
-
         pair01 = factors.tile([P, R, R, PASSES * PACK], F32)
         nc.vector.tensor_tensor(
             out=pair01[:],
@@ -98,7 +93,7 @@ def tile_fast_tucker_taylor_pa_s_kernel(tc, z, G2, grad_out, out):
             in1=z1.unsqueeze(2).to_broadcast([P, R, R, PASSES * PACK]),
             op=MULT,
         )
-
+        kron_grouped = []
         for g in range(PASSES):
             t_cols = slice(g * PACK, (g + 1) * PACK)
             kron = per_pass.tile([P, R, R * R, PACK], BF16, name="kron", align_bytes=64)
@@ -108,18 +103,27 @@ def tile_fast_tucker_taylor_pa_s_kernel(tc, z, G2, grad_out, out):
                 in1=z2[:, :, t_cols].unsqueeze(2).to_broadcast([P, R, R * R, PACK]),
                 op=MULT,
             )
-            nc.vector.quantize_mx(
-                out=grad_codes[:, g, :].bitcast(E5M2_X4),
-                scales=grad_scales[:, g, :],
-                in_=grad_grouped[g][:],
-            )
+            kron_grouped.append(kron)
+
+        kron_codes = operands.tile([P, PASSES, K], U32, align_bytes=64)
+        kron_scales = operands.tile([P, PASSES, K], U8, align_bytes=64)
+        grad_codes = operands.tile([P, PASSES, Q], U32, align_bytes=64)
+        grad_scales = operands.tile([P, PASSES, Q], U8, align_bytes=64)
+        acc = [psum_acc.tile([P, K], F32, name="acc%d" % i) for i in range(Q_TILES)]
+
+        for g in range(PASSES):
             nc.vector.quantize_mx(
                 out=kron_codes[:, g, :].bitcast(E4M3_X4),
                 scales=kron_scales[:, g, :],
-                in_=kron[:].rearrange("p c w t -> p (c w t)"),
+                in_=kron_grouped[g][:].rearrange("p c w t -> p (c w t)"),
             )
             for i in range(Q_TILES):
                 q_cols = slice(i * P, (i + 1) * P)
+                nc.vector.quantize_mx(
+                    out=grad_codes[:, g, q_cols].bitcast(E5M2_X4),
+                    scales=grad_scales[:, g, q_cols],
+                    in_=grad_grouped[g][:, i * P * PACK : (i + 1) * P * PACK],
+                )
                 nc.tensor.matmul_mx(
                     out=acc[i][:],
                     lhsT=grad_codes[:, g, q_cols].bitcast(E5M2_X4),

@@ -24,6 +24,8 @@ PASSES = B // K_PASS
 Q_TILES = Q // P
 CHUNKS = PASSES * HALVES
 
+VECTOR_C = 6
+
 FLOPS = 2 * Q * K * B
 BYTES = ORD * R * B * 2 + Q * B * 2 + Q * K * 4
 
@@ -67,6 +69,7 @@ def tile_fast_tucker_taylor_pa_s_kernel(tc, z, G2, grad_out, out):
         z0 = z_f32[:, 0:R, :]
         z1 = z_f32[:, R : 2 * R, :]
         z2 = z_f32[:, 3 * R : 4 * R, :]
+        z2_psum = z_cols[:].bitcast(BF16).rearrange("p (r i) -> p r i", i=PASSES * PACK)[:, 3 * R : 4 * R, :]
 
         grad_grouped = []
         for g in range(PASSES):
@@ -97,10 +100,17 @@ def tile_fast_tucker_taylor_pa_s_kernel(tc, z, G2, grad_out, out):
         for g in range(PASSES):
             t_cols = slice(g * PACK, (g + 1) * PACK)
             kron = per_pass.tile([P, R, R * R, PACK], BF16, name="kron", align_bytes=64)
+            pair = pair01[:, :, :, t_cols].rearrange("p b a t -> p (b a) t").unsqueeze(1)
             nc.vector.tensor_tensor(
-                out=kron[:],
-                in0=pair01[:, :, :, t_cols].rearrange("p b a t -> p (b a) t").unsqueeze(1).to_broadcast([P, R, R * R, PACK]),
-                in1=z2[:, :, t_cols].unsqueeze(2).to_broadcast([P, R, R * R, PACK]),
+                out=kron[:, 0:VECTOR_C],
+                in0=pair.to_broadcast([P, VECTOR_C, R * R, PACK]),
+                in1=z2_psum[:, 0:VECTOR_C, t_cols].unsqueeze(2).to_broadcast([P, VECTOR_C, R * R, PACK]),
+                op=MULT,
+            )
+            nc.gpsimd.tensor_tensor(
+                out=kron[:, VECTOR_C:R],
+                in0=pair.to_broadcast([P, R - VECTOR_C, R * R, PACK]),
+                in1=z2[:, VECTOR_C:R, t_cols].unsqueeze(2).to_broadcast([P, R - VECTOR_C, R * R, PACK]),
                 op=MULT,
             )
             kron_grouped.append(kron)

@@ -24,8 +24,6 @@ PASSES = B // K_PASS
 Q_TILES = Q // P
 CHUNKS = PASSES * HALVES
 
-VECTOR_C = 6
-
 FLOPS = 2 * Q * K * B
 BYTES = ORD * R * B * 2 + Q * B * 2 + Q * K * 4
 
@@ -96,44 +94,48 @@ def tile_fast_tucker_taylor_pa_s_kernel(tc, z, G2, grad_out, out):
             in1=z1.unsqueeze(2).to_broadcast([P, R, R, PASSES * PACK]),
             op=MULT,
         )
-        kron_grouped = []
-        for g in range(PASSES):
-            t_cols = slice(g * PACK, (g + 1) * PACK)
-            kron = per_pass.tile([P, R, R * R, PACK], BF16, name="kron", align_bytes=64)
-            pair = pair01[:, :, :, t_cols].rearrange("p b a t -> p (b a) t").unsqueeze(1)
-            nc.vector.tensor_tensor(
-                out=kron[:, 0:VECTOR_C],
-                in0=pair.to_broadcast([P, VECTOR_C, R * R, PACK]),
-                in1=z2_psum[:, 0:VECTOR_C, t_cols].unsqueeze(2).to_broadcast([P, VECTOR_C, R * R, PACK]),
-                op=MULT,
-            )
-            nc.gpsimd.tensor_tensor(
-                out=kron[:, VECTOR_C:R],
-                in0=pair.to_broadcast([P, R - VECTOR_C, R * R, PACK]),
-                in1=z2[:, VECTOR_C:R, t_cols].unsqueeze(2).to_broadcast([P, R - VECTOR_C, R * R, PACK]),
-                op=MULT,
-            )
-            kron_grouped.append(kron)
-
         kron_codes = operands.tile([P, PASSES, K], U32, align_bytes=64)
         kron_scales = operands.tile([P, PASSES, K], U8, align_bytes=64)
         grad_codes = operands.tile([P, PASSES, Q], U32, align_bytes=64)
         grad_scales = operands.tile([P, PASSES, Q], U8, align_bytes=64)
         acc = [psum_acc.tile([P, K], F32, name="acc%d" % i) for i in range(Q_TILES)]
 
+        def build_kron(engine, kron, g, c_from, c_to, z2_view):
+            t_cols = slice(g * PACK, (g + 1) * PACK)
+            shape = [P, c_to - c_from, R * R, PACK]
+            engine.tensor_tensor(
+                out=kron[:, c_from:c_to],
+                in0=pair01[:, :, :, t_cols].rearrange("p b a t -> p (b a) t").unsqueeze(1).to_broadcast(shape),
+                in1=z2_view[:, c_from:c_to, t_cols].unsqueeze(2).to_broadcast(shape),
+                op=MULT,
+            )
+
+        def quantise_grad(g, i):
+            q_cols = slice(i * P, (i + 1) * P)
+            nc.vector.quantize_mx(
+                out=grad_codes[:, g, q_cols].bitcast(E5M2_X4),
+                scales=grad_scales[:, g, q_cols],
+                in_=grad_grouped[g][:, i * P * PACK : (i + 1) * P * PACK],
+            )
+
+        kron_grouped = [
+            per_pass.tile([P, R, R * R, PACK], BF16, name="kron", align_bytes=64) for g in range(PASSES)
+        ]
+        build_kron(nc.gpsimd, kron_grouped[PASSES - 1], PASSES - 1, R // 2, R, z2)
+
         for g in range(PASSES):
+            vector_c = R // 2 if g == PASSES - 1 else R
+            build_kron(nc.vector, kron_grouped[g], g, 0, vector_c, z2_psum)
+            quantise_grad(g, 0)
             nc.vector.quantize_mx(
                 out=kron_codes[:, g, :].bitcast(E4M3_X4),
                 scales=kron_scales[:, g, :],
                 in_=kron_grouped[g][:].rearrange("p c w t -> p (c w t)"),
             )
+            for i in range(1, Q_TILES):
+                quantise_grad(g, i)
             for i in range(Q_TILES):
                 q_cols = slice(i * P, (i + 1) * P)
-                nc.vector.quantize_mx(
-                    out=grad_codes[:, g, q_cols].bitcast(E5M2_X4),
-                    scales=grad_scales[:, g, q_cols],
-                    in_=grad_grouped[g][:, i * P * PACK : (i + 1) * P * PACK],
-                )
                 nc.tensor.matmul_mx(
                     out=acc[i][:],
                     lhsT=grad_codes[:, g, q_cols].bitcast(E5M2_X4),

@@ -10,6 +10,7 @@ U8 = mybir.dt.uint8
 E4M3_X4 = mybir.dt.float8_e4m3fn_x4
 E5M2_X4 = mybir.dt.float8_e5m2_x4
 MULT = mybir.AluOpType.mult
+COPY = mybir.ActivationFunctionType.Copy
 
 P = 128
 PACK = 4
@@ -23,6 +24,11 @@ K = R**ORD
 PASSES = B // K_PASS
 Q_TILES = Q // P
 CHUNKS = PASSES * HALVES
+
+LAST = PASSES - 1
+GPSIMD_C = R // 2
+SCALAR_C = PASSES
+VECTOR_C = R - GPSIMD_C - SCALAR_C
 
 FLOPS = 2 * Q * K * B
 BYTES = ORD * R * B * 2 + Q * B * 2 + Q * K * 4
@@ -62,15 +68,50 @@ def tile_fast_tucker_taylor_pa_s_kernel(tc, z, G2, grad_out, out):
 
         z_cols = psum_z.tile([P, P], F32)
         nc.tensor.transpose(z_cols[:], z_rows[:].bitcast(F32), identity[:])
-        z_f32 = factors.tile([P, 4 * R, PASSES * PACK], F32)
-        nc.vector.tensor_copy(out=z_f32[:].rearrange("p r i -> p (r i)"), in_=z_cols[:].bitcast(BF16))
-        z0 = z_f32[:, 0:R, :]
-        z1 = z_f32[:, R : 2 * R, :]
-        z2 = z_f32[:, 3 * R : 4 * R, :]
-        z2_psum = z_cols[:].bitcast(BF16).rearrange("p (r i) -> p r i", i=PASSES * PACK)[:, 3 * R : 4 * R, :]
+        z_pairs = z_cols[:].bitcast(BF16).rearrange("p (s r i) -> p s r i", s=4, r=R)
+        z0_psum = z_pairs[:, 0]
+        z2_psum = z_pairs[:, 3]
+        z12 = factors.tile([P, 2, R, PASSES * PACK], F32)
+        nc.vector.tensor_copy(out=z12[:], in_=z_pairs[:, 2:4])
+        z1 = z12[:, 0]
+        z2 = z12[:, 1]
+
+        pair01 = [per_pass.tile([P, R, R, PACK], F32, name="pair01") for g in range(PASSES)]
+        for g in reversed(range(PASSES)):
+            t_cols = slice(g * PACK, (g + 1) * PACK)
+            nc.vector.tensor_tensor(
+                out=pair01[g][:],
+                in0=z0_psum[:, :, t_cols].unsqueeze(1).to_broadcast([P, R, R, PACK]),
+                in1=z1[:, :, t_cols].unsqueeze(2).to_broadcast([P, R, R, PACK]),
+                op=MULT,
+            )
+
+        kron = [per_pass.tile([P, R, R * R, PACK], BF16, name="kron", align_bytes=64) for g in range(PASSES)]
+
+        def build_kron(engine, g, c_from, c_to, z2_view):
+            t_cols = slice(g * PACK, (g + 1) * PACK)
+            shape = [P, c_to - c_from, R * R, PACK]
+            engine.tensor_tensor(
+                out=kron[g][:, c_from:c_to],
+                in0=pair01[g][:].rearrange("p b a t -> p (b a) t").unsqueeze(1).to_broadcast(shape),
+                in1=z2_view[:, c_from:c_to, t_cols].unsqueeze(2).to_broadcast(shape),
+                op=MULT,
+            )
+
+        def build_kron_on_scalar(g, c):
+            for t in range(PACK):
+                nc.scalar.activation(
+                    out=kron[g][:, c, :, t],
+                    in_=pair01[g][:, :, :, t].rearrange("p b a -> p (b a)"),
+                    func=COPY,
+                    scale=z2[:, c, g * PACK + t : g * PACK + t + 1],
+                )
+
+        build_kron(nc.gpsimd, LAST, R - GPSIMD_C, R, z2)
 
         grad_grouped = []
         for g in range(PASSES):
+            build_kron_on_scalar(LAST, VECTOR_C + g)
             grouped = per_pass.tile([P, Q_TILES * P * PACK], BF16, name="grad_grouped", align_bytes=64)
             grouped_words = grouped[:].bitcast(F32).rearrange(
                 "p (i q u) -> p i q u", i=Q_TILES, u=HALVES
@@ -87,28 +128,11 @@ def tile_fast_tucker_taylor_pa_s_kernel(tc, z, G2, grad_out, out):
                 )
             grad_grouped.append(grouped)
 
-        pair01 = factors.tile([P, R, R, PASSES * PACK], F32)
-        nc.vector.tensor_tensor(
-            out=pair01[:],
-            in0=z0.unsqueeze(1).to_broadcast([P, R, R, PASSES * PACK]),
-            in1=z1.unsqueeze(2).to_broadcast([P, R, R, PASSES * PACK]),
-            op=MULT,
-        )
         kron_codes = operands.tile([P, PASSES, K], U32, align_bytes=64)
         kron_scales = operands.tile([P, PASSES, K], U8, align_bytes=64)
         grad_codes = operands.tile([P, PASSES, Q], U32, align_bytes=64)
         grad_scales = operands.tile([P, PASSES, Q], U8, align_bytes=64)
         acc = [psum_acc.tile([P, K], F32, name="acc%d" % i) for i in range(Q_TILES)]
-
-        def build_kron(engine, kron, g, c_from, c_to, z2_view):
-            t_cols = slice(g * PACK, (g + 1) * PACK)
-            shape = [P, c_to - c_from, R * R, PACK]
-            engine.tensor_tensor(
-                out=kron[:, c_from:c_to],
-                in0=pair01[:, :, :, t_cols].rearrange("p b a t -> p (b a) t").unsqueeze(1).to_broadcast(shape),
-                in1=z2_view[:, c_from:c_to, t_cols].unsqueeze(2).to_broadcast(shape),
-                op=MULT,
-            )
 
         def quantise_grad(g, i):
             q_cols = slice(i * P, (i + 1) * P)
@@ -118,19 +142,13 @@ def tile_fast_tucker_taylor_pa_s_kernel(tc, z, G2, grad_out, out):
                 in_=grad_grouped[g][:, i * P * PACK : (i + 1) * P * PACK],
             )
 
-        kron_grouped = [
-            per_pass.tile([P, R, R * R, PACK], BF16, name="kron", align_bytes=64) for g in range(PASSES)
-        ]
-        build_kron(nc.gpsimd, kron_grouped[PASSES - 1], PASSES - 1, R // 2, R, z2)
-
         for g in range(PASSES):
-            vector_c = R // 2 if g == PASSES - 1 else R
-            build_kron(nc.vector, kron_grouped[g], g, 0, vector_c, z2_psum)
+            build_kron(nc.vector, g, 0, VECTOR_C if g == LAST else R, z2_psum)
             quantise_grad(g, 0)
             nc.vector.quantize_mx(
                 out=kron_codes[:, g, :].bitcast(E4M3_X4),
                 scales=kron_scales[:, g, :],
-                in_=kron_grouped[g][:].rearrange("p c w t -> p (c w t)"),
+                in_=kron[g][:].rearrange("p c w t -> p (c w t)"),
             )
             for i in range(1, Q_TILES):
                 quantise_grad(g, i)
@@ -143,7 +161,7 @@ def tile_fast_tucker_taylor_pa_s_kernel(tc, z, G2, grad_out, out):
                     rhs=kron_codes[:, g, :].bitcast(E4M3_X4),
                     rhs_scale=kron_scales[:, g, :],
                     start=(g == 0),
-                    stop=(g == PASSES - 1),
+                    stop=(g == LAST),
                 )
 
         for i in range(Q_TILES):

@@ -30,6 +30,8 @@ GPSIMD_C = R // 2
 SCALAR_C = PASSES
 VECTOR_C = R - GPSIMD_C - SCALAR_C
 
+WARM_UPS = 3
+
 FLOPS = 2 * Q * K * B
 BYTES = ORD * R * B * 2 + Q * B * 2 + Q * K * 4
 
@@ -43,7 +45,8 @@ def tile_fast_tucker_taylor_pa_s_kernel(tc, z, G2, grad_out, out):
         operands = stack.enter_context(tc.tile_pool(name="operands", bufs=1))
         results = stack.enter_context(tc.tile_pool(name="results", bufs=Q_TILES))
         psum_z = stack.enter_context(tc.psum_pool(name="psum_z", bufs=1))
-        psum_t = stack.enter_context(tc.psum_pool(name="psum_t", bufs=3))
+        psum_t = stack.enter_context(tc.psum_pool(name="psum_t", bufs=2))
+        psum_w = stack.enter_context(tc.psum_pool(name="psum_w", bufs=1))
         psum_acc = stack.enter_context(tc.psum_pool(name="psum_acc", bufs=1))
         stack.enter_context(tc.manual_schedule())
 
@@ -68,6 +71,14 @@ def tile_fast_tucker_taylor_pa_s_kernel(tc, z, G2, grad_out, out):
 
         z_cols = psum_z.tile([P, P], F32)
         nc.tensor.transpose(z_cols[:], z_rows[:].bitcast(F32), identity[:])
+
+        unread = psum_w.tile([P, P], F32)
+
+        def keep_tensor_busy():
+            for d in range(WARM_UPS):
+                nc.tensor.matmul(unread[:], lhsT=identity[:], rhs=identity[:], start=True, stop=True)
+
+        keep_tensor_busy()
         z_pairs = z_cols[:].bitcast(BF16).rearrange("p (s r i) -> p s r i", s=4, r=R)
         z0_psum = z_pairs[:, 0]
         z2_psum = z_pairs[:, 3]
@@ -127,6 +138,7 @@ def tile_fast_tucker_taylor_pa_s_kernel(tc, z, G2, grad_out, out):
                     in_=bank[:].rearrange("p i u q -> p i q u"),
                 )
             grad_grouped.append(grouped)
+            keep_tensor_busy()
 
         kron_codes = operands.tile([P, PASSES, K], U32, align_bytes=64)
         kron_scales = operands.tile([P, PASSES, K], U8, align_bytes=64)

@@ -154,32 +154,44 @@ def tile_fast_tucker_taylor_pa_s_kernel(tc, z, G2, grad_out, out):
                 in_=grad_grouped[g][:, i * P * PACK : (i + 1) * P * PACK],
             )
 
-        for g in range(PASSES):
-            build_kron(nc.vector, g, 0, VECTOR_C if g == LAST else R, z2_psum)
-            quantise_grad(g, 0)
+        def quantise_kron(g):
             nc.vector.quantize_mx(
                 out=kron_codes[:, g, :].bitcast(E4M3_X4),
                 scales=kron_scales[:, g, :],
                 in_=kron[g][:].rearrange("p c w t -> p (c w t)"),
             )
-            for i in range(1, Q_TILES):
-                quantise_grad(g, i)
-            for i in range(Q_TILES):
-                q_cols = slice(i * P, (i + 1) * P)
-                nc.tensor.matmul_mx(
-                    out=acc[i][:],
-                    lhsT=grad_codes[:, g, q_cols].bitcast(E5M2_X4),
-                    lhsT_scale=grad_scales[:, g, q_cols],
-                    rhs=kron_codes[:, g, :].bitcast(E4M3_X4),
-                    rhs_scale=kron_scales[:, g, :],
-                    start=(g == 0),
-                    stop=(g == LAST),
-                )
 
-        for i in range(Q_TILES):
+        def multiply(g, i):
+            q_cols = slice(i * P, (i + 1) * P)
+            nc.tensor.matmul_mx(
+                out=acc[i][:],
+                lhsT=grad_codes[:, g, q_cols].bitcast(E5M2_X4),
+                lhsT_scale=grad_scales[:, g, q_cols],
+                rhs=kron_codes[:, g, :].bitcast(E4M3_X4),
+                rhs_scale=kron_scales[:, g, :],
+                start=(g == 0),
+                stop=(g == LAST),
+            )
+
+        def store(i, engine_copy, pieces):
             result = results.tile([P, K], F32, name="result")
-            if i % 2 == 0:
-                nc.scalar.copy(out=result[:], in_=acc[i][:])
-            else:
-                nc.vector.tensor_copy(out=result[:], in_=acc[i][:])
-            nc.sync.dma_start(out=out[i * P : (i + 1) * P, :], in_=result[:])
+            width = K // pieces
+            for h in range(pieces):
+                cols = slice(h * width, (h + 1) * width)
+                engine_copy(out=result[:, cols], in_=acc[i][:, cols])
+                nc.sync.dma_start(out=out[i * P : (i + 1) * P, cols], in_=result[:, cols])
+
+        for g in range(PASSES):
+            build_kron(nc.vector, g, 0, VECTOR_C if g == LAST else R, z2_psum)
+            quantise_grad(g, 0)
+            quantise_kron(g)
+            multiply(g, 0)
+            if g != LAST:
+                keep_tensor_busy()
+        store(0, nc.scalar.copy, 1)
+        for i in range(1, Q_TILES):
+            for g in range(PASSES):
+                quantise_grad(g, i)
+                multiply(g, i)
+        for i in range(1, Q_TILES):
+            store(i, nc.vector.tensor_copy if i == 2 else nc.scalar.copy, 1)

@@ -46,16 +46,18 @@ def tile_fast_tucker_taylor_pa_s_kernel(tc, z, G2, grad_out, out):
         results = stack.enter_context(tc.tile_pool(name="results", bufs=Q_TILES))
         psum_z = stack.enter_context(tc.psum_pool(name="psum_z", bufs=1))
         psum_t = stack.enter_context(tc.psum_pool(name="psum_t", bufs=2))
-        psum_w = stack.enter_context(tc.psum_pool(name="psum_w", bufs=1))
         psum_acc = stack.enter_context(tc.psum_pool(name="psum_acc", bufs=1))
         stack.enter_context(tc.manual_schedule())
 
         z_runs = z.rearrange("j r (h w) -> (j r h) w", h=CHUNKS)
         runs_of_two = 2 * R * CHUNKS
         runs_of_one = R * CHUNKS
-        z_rows = factors.tile([P, P * PAIR], BF16)
-        nc.sync.dma_start(out=z_rows[0:runs_of_two, :], in_=z_runs[0:runs_of_two, :])
-        nc.sync.dma_start(out=z_rows[runs_of_two:P, :], in_=z_runs[runs_of_one : runs_of_one + runs_of_two, :])
+        z_rows_01 = factors.tile([P, P * PAIR], BF16)
+        z_rows_12 = factors.tile([P, P * PAIR], BF16)
+        nc.vector.memset(z_rows_01[runs_of_two:P, :], 0.0)
+        nc.vector.memset(z_rows_12[0:runs_of_two, :], 0.0)
+        nc.sync.dma_start(out=z_rows_01[0:runs_of_two, :], in_=z_runs[0:runs_of_two, :])
+        nc.sync.dma_start(out=z_rows_12[runs_of_two:P, :], in_=z_runs[runs_of_one : runs_of_one + runs_of_two, :])
 
         grad_rows = []
         for g in range(PASSES):
@@ -69,23 +71,29 @@ def tile_fast_tucker_taylor_pa_s_kernel(tc, z, G2, grad_out, out):
         identity = consts.tile([P, P], F32)
         make_identity(nc, identity[:])
 
-        z_cols = psum_z.tile([P, P], F32)
-        nc.tensor.transpose(z_cols[:], z_rows[:].bitcast(F32), identity[:])
+        z_cols_01 = psum_z.tile([P, P], F32)
+        nc.tensor.transpose(z_cols_01[:], z_rows_01[:].bitcast(F32), identity[:])
+        z_cols_12 = psum_z.tile([P, P], F32)
+        nc.tensor.transpose(z_cols_12[:], z_rows_12[:].bitcast(F32), identity[:])
 
-        unread = psum_w.tile([P, P], F32)
+        acc = [psum_acc.tile([P, K], F32, name="acc%d" % i) for i in range(Q_TILES)]
+        unread = acc[Q_TILES - 1][:, 0:P]
 
         def keep_tensor_busy():
             for d in range(WARM_UPS):
-                nc.tensor.matmul(unread[:], lhsT=identity[:], rhs=identity[:], start=True, stop=True)
+                nc.tensor.matmul(unread, lhsT=identity[:], rhs=identity[:], start=True, stop=True)
 
         keep_tensor_busy()
-        z_pairs = z_cols[:].bitcast(BF16).rearrange("p (s r i) -> p s r i", s=4, r=R)
-        z0_psum = z_pairs[:, 0]
-        z2_psum = z_pairs[:, 3]
-        z12 = factors.tile([P, 2, R, PASSES * PACK], F32)
-        nc.vector.tensor_copy(out=z12[:], in_=z_pairs[:, 2:4])
-        z1 = z12[:, 0]
-        z2 = z12[:, 1]
+        z_pairs_01 = z_cols_01[:].bitcast(BF16).rearrange("p (s r i) -> p s r i", s=4, r=R)
+        z_pairs_12 = z_cols_12[:].bitcast(BF16).rearrange("p (s r i) -> p s r i", s=4, r=R)
+        z0_psum = z_pairs_01[:, 0]
+        z2_psum = z_pairs_12[:, 3]
+        z1_tile = factors.tile([P, R, PASSES * PACK], F32)
+        nc.vector.tensor_copy(out=z1_tile[:], in_=z_pairs_01[:, 1])
+        z2_tile = factors.tile([P, R, PASSES * PACK], F32)
+        nc.scalar.copy(out=z2_tile[:], in_=z_pairs_12[:, 3])
+        z1 = z1_tile[:]
+        z2 = z2_tile[:]
 
         pair01 = [per_pass.tile([P, R, R, PACK], F32, name="pair01") for g in range(PASSES)]
         for g in reversed(range(PASSES)):
@@ -144,7 +152,6 @@ def tile_fast_tucker_taylor_pa_s_kernel(tc, z, G2, grad_out, out):
         kron_scales = operands.tile([P, PASSES, K], U8, align_bytes=64)
         grad_codes = operands.tile([P, PASSES, Q], U32, align_bytes=64)
         grad_scales = operands.tile([P, PASSES, Q], U8, align_bytes=64)
-        acc = [psum_acc.tile([P, K], F32, name="acc%d" % i) for i in range(Q_TILES)]
 
         def quantise_grad(g, i):
             q_cols = slice(i * P, (i + 1) * P)

@@ -190,11 +190,10 @@ def tile_fast_tucker_taylor_pa_s_kernel(tc, z, G2, grad_out, out):
 
         for g in range(PASSES):
             build_kron(nc.vector, g, 0, VECTOR_C if g == LAST else R, z2_psum)
+        for g in range(PASSES):
             quantise_grad(g, 0)
             quantise_kron(g)
             multiply(g, 0)
-            if g != LAST:
-                keep_tensor_busy()
         store(0, nc.scalar.copy, 1)
         for i in range(1, Q_TILES):
             for g in range(PASSES):

@@ -44,8 +44,8 @@ def tile_fast_tucker_taylor_pa_s_kernel(tc, z, G2, grad_out, out):
         per_pass = stack.enter_context(tc.tile_pool(name="per_pass", bufs=PASSES))
         operands = stack.enter_context(tc.tile_pool(name="operands", bufs=1))
         results = stack.enter_context(tc.tile_pool(name="results", bufs=Q_TILES))
-        psum_z = stack.enter_context(tc.psum_pool(name="psum_z", bufs=1))
-        psum_t = stack.enter_context(tc.psum_pool(name="psum_t", bufs=2))
+        psum_z = stack.enter_context(tc.psum_pool(name="psum_z", bufs=2))
+        psum_t = stack.enter_context(tc.psum_pool(name="psum_t", bufs=4))
         psum_acc = stack.enter_context(tc.psum_pool(name="psum_acc", bufs=1))
         stack.enter_context(tc.manual_schedule())
 
@@ -60,32 +60,34 @@ def tile_fast_tucker_taylor_pa_s_kernel(tc, z, G2, grad_out, out):
         nc.sync.dma_start(out=z_rows_12[runs_of_two:P, :], in_=z_runs[runs_of_one : runs_of_one + runs_of_two, :])
 
         grad_rows = []
-        for g in range(PASSES):
-            rows = per_pass.tile([P, Q_TILES, K_PASS], BF16, name="grad_rows")
+        for half in range(2):
+            rows = per_pass.tile([P, 2, B], BF16, name="grad_rows")
             nc.sync.dma_start(
                 out=rows[:],
-                in_=grad_out[:, g * K_PASS : (g + 1) * K_PASS].rearrange("(i p) n -> p i n", p=P),
+                in_=grad_out[half * 2 * P : (half + 1) * 2 * P, :].rearrange("(j p) n -> p j n", p=P),
             )
             grad_rows.append(rows)
 
         identity = consts.tile([P, P], F32)
         make_identity(nc, identity[:])
 
-        z_cols_01 = psum_z.tile([P, P], F32)
-        nc.tensor.transpose(z_cols_01[:], z_rows_01[:].bitcast(F32), identity[:])
-        z_cols_12 = psum_z.tile([P, P], F32)
-        nc.tensor.transpose(z_cols_12[:], z_rows_12[:].bitcast(F32), identity[:])
+        z_bank_01 = psum_z.tile([P, K], F32, name="z_bank")
+        z_cols_01 = z_bank_01[:, 0:P]
+        nc.tensor.transpose(z_cols_01, z_rows_01[:].bitcast(F32), identity[:])
+        z_bank_12 = psum_z.tile([P, K], F32, name="z_bank")
+        z_cols_12 = z_bank_12[:, 0:P]
+        nc.tensor.transpose(z_cols_12, z_rows_12[:].bitcast(F32), identity[:])
 
-        acc = [psum_acc.tile([P, K], F32, name="acc%d" % i) for i in range(Q_TILES)]
-        unread = acc[Q_TILES - 1][:, 0:P]
+        acc = [psum_acc.tile([P, K], F32, name="acc%d" % i) for i in range(2)]
+        unread = acc[1][:, 0:P]
 
         def keep_tensor_busy():
             for d in range(WARM_UPS):
                 nc.tensor.matmul(unread, lhsT=identity[:], rhs=identity[:], start=True, stop=True)
 
         keep_tensor_busy()
-        z_pairs_01 = z_cols_01[:].bitcast(BF16).rearrange("p (s r i) -> p s r i", s=4, r=R)
-        z_pairs_12 = z_cols_12[:].bitcast(BF16).rearrange("p (s r i) -> p s r i", s=4, r=R)
+        z_pairs_01 = z_cols_01.bitcast(BF16).rearrange("p (s r i) -> p s r i", s=4, r=R)
+        z_pairs_12 = z_cols_12.bitcast(BF16).rearrange("p (s r i) -> p s r i", s=4, r=R)
         z0_psum = z_pairs_01[:, 0]
         z2_psum = z_pairs_12[:, 3]
         z1_tile = factors.tile([P, R, PASSES * PACK], F32)
@@ -128,24 +130,23 @@ def tile_fast_tucker_taylor_pa_s_kernel(tc, z, G2, grad_out, out):
 
         build_kron(nc.gpsimd, LAST, R - GPSIMD_C, R, z2)
 
-        grad_grouped = []
-        for g in range(PASSES):
-            build_kron_on_scalar(LAST, VECTOR_C + g)
-            grouped = per_pass.tile([P, Q_TILES * P * PACK], BF16, name="grad_grouped", align_bytes=64)
-            grouped_words = grouped[:].bitcast(F32).rearrange(
-                "p (i q u) -> p i q u", i=Q_TILES, u=HALVES
-            )
-            for first in range(0, Q_TILES, 2):
+        grad_grouped = [
+            per_pass.tile([P, Q_TILES * P * PACK], BF16, name="grad_grouped", align_bytes=64) for g in range(PASSES)
+        ]
+        for half in range(2):
+            build_kron_on_scalar(LAST, VECTOR_C + half)
+            for g in range(PASSES):
+                grouped_words = grad_grouped[g][:].bitcast(F32).rearrange("p (i q u) -> p i q u", i=Q_TILES, u=HALVES)
                 bank = psum_t.tile([P, 2, HALVES, P], F32, name="bank")
-                for i in range(2):
-                    words = grad_rows[g][:, first + i, :].bitcast(F32)
+                for j in range(2):
+                    words = grad_rows[half][:, j, :].bitcast(F32)
                     for u in range(HALVES):
-                        nc.tensor.transpose(bank[:, i, u, :], words[:, u * P : (u + 1) * P], identity[:])
+                        chunk = g * HALVES + u
+                        nc.tensor.transpose(bank[:, j, u, :], words[:, chunk * P : (chunk + 1) * P], identity[:])
                 nc.scalar.copy(
-                    out=grouped_words[:, first : first + 2],
+                    out=grouped_words[:, 2 * half : 2 * half + 2],
                     in_=bank[:].rearrange("p i u q -> p i q u"),
                 )
-            grad_grouped.append(grouped)
             keep_tensor_busy()
 
         kron_codes = operands.tile([P, PASSES, K], U32, align_bytes=64)
@@ -190,6 +191,7 @@ def tile_fast_tucker_taylor_pa_s_kernel(tc, z, G2, grad_out, out):
 
         for g in range(PASSES):
             build_kron(nc.vector, g, 0, VECTOR_C if g == LAST else R, z2_psum)
+        acc.extend([psum_z.tile([P, K], F32, name="z_bank") for i in range(2, Q_TILES)])
         for g in range(PASSES):
             quantise_grad(g, 0)
             quantise_kron(g)

@@ -189,11 +189,12 @@ def tile_fast_tucker_taylor_pa_s_kernel(tc, z, G2, grad_out, out):
                 engine_copy(out=result[:, cols], in_=acc[i][:, cols])
                 nc.sync.dma_start(out=out[i * P : (i + 1) * P, cols], in_=result[:, cols])
 
-        for g in range(PASSES):
+        for g in reversed(range(PASSES)):
             build_kron(nc.vector, g, 0, VECTOR_C if g == LAST else R, z2_psum)
         acc.extend([psum_z.tile([P, K], F32, name="z_bank") for i in range(2, Q_TILES)])
         for g in range(PASSES):
             quantise_grad(g, 0)
+        for g in range(PASSES):
             quantise_kron(g)
             multiply(g, 0)
         store(0, nc.scalar.copy, 1)

@@ -26,9 +26,8 @@ Q_TILES = Q // P
 CHUNKS = PASSES * HALVES
 
 LAST = PASSES - 1
-GPSIMD_C = R // 2
-SCALAR_C = PASSES
-VECTOR_C = R - GPSIMD_C - SCALAR_C
+SCALAR_C = 2
+VECTOR_B = 2
 
 WARM_UPS = 3
 
@@ -109,13 +108,13 @@ def tile_fast_tucker_taylor_pa_s_kernel(tc, z, G2, grad_out, out):
 
         kron = [per_pass.tile([P, R, R * R, PACK], BF16, name="kron", align_bytes=64) for g in range(PASSES)]
 
-        def build_kron(engine, g, c_from, c_to, z2_view):
+        def build_kron(engine, g, c_from, b_from, b_to, z2_view):
             t_cols = slice(g * PACK, (g + 1) * PACK)
-            shape = [P, c_to - c_from, R * R, PACK]
+            shape = [P, R - c_from, (b_to - b_from) * R, PACK]
             engine.tensor_tensor(
-                out=kron[g][:, c_from:c_to],
-                in0=pair01[g][:].rearrange("p b a t -> p (b a) t").unsqueeze(1).to_broadcast(shape),
-                in1=z2_view[:, c_from:c_to, t_cols].unsqueeze(2).to_broadcast(shape),
+                out=kron[g][:, c_from:, b_from * R : b_to * R],
+                in0=pair01[g][:, b_from:b_to].rearrange("p b a t -> p (b a) t").unsqueeze(1).to_broadcast(shape),
+                in1=z2_view[:, c_from:, t_cols].unsqueeze(2).to_broadcast(shape),
                 op=MULT,
             )
 
@@ -128,13 +127,13 @@ def tile_fast_tucker_taylor_pa_s_kernel(tc, z, G2, grad_out, out):
                     scale=z2[:, c, g * PACK + t : g * PACK + t + 1],
                 )
 
-        build_kron(nc.gpsimd, LAST, R - GPSIMD_C, R, z2)
+        build_kron(nc.gpsimd, LAST, SCALAR_C, VECTOR_B, R, z2)
 
         grad_grouped = [
             per_pass.tile([P, Q_TILES * P * PACK], BF16, name="grad_grouped", align_bytes=64) for g in range(PASSES)
         ]
         for half in range(2):
-            build_kron_on_scalar(LAST, VECTOR_C + half)
+            build_kron_on_scalar(LAST, half)
             for g in range(PASSES):
                 grouped_words = grad_grouped[g][:].bitcast(F32).rearrange("p (i q u) -> p i q u", i=Q_TILES, u=HALVES)
                 bank = psum_t.tile([P, 2, HALVES, P], F32, name="bank")
@@ -189,8 +188,8 @@ def tile_fast_tucker_taylor_pa_s_kernel(tc, z, G2, grad_out, out):
                 engine_copy(out=result[:, cols], in_=acc[i][:, cols])
                 nc.sync.dma_start(out=out[i * P : (i + 1) * P, cols], in_=result[:, cols])
 
-        for g in reversed(range(PASSES)):
-            build_kron(nc.vector, g, 0, VECTOR_C if g == LAST else R, z2_psum)
+        build_kron(nc.vector, LAST, SCALAR_C, 0, VECTOR_B, z2_psum)
+        build_kron(nc.vector, 0, 0, 0, R, z2_psum)
         acc.extend([psum_z.tile([P, K], F32, name="z_bank") for i in range(2, Q_TILES)])
         for g in range(PASSES):
             quantise_grad(g, 0)

@@ -29,7 +29,7 @@ LAST = PASSES - 1
 SCALAR_C = 2
 VECTOR_B = 2
 
-WARM_UPS = 3
+WARM_UPS = 2
 
 FLOPS = 2 * Q * K * B
 BYTES = ORD * R * B * 2 + Q * B * 2 + Q * K * 4
@@ -190,6 +190,8 @@ def tile_fast_tucker_taylor_pa_s_kernel(tc, z, G2, grad_out, out):
 
         build_kron(nc.vector, LAST, SCALAR_C, 0, VECTOR_B, z2_psum)
         build_kron(nc.vector, 0, 0, 0, R, z2_psum)
+        kron_columns = kron[0][:].rearrange("p c w t -> p (c w t)")
+        nc.tensor.matmul(acc[1][:], lhsT=kron_columns[:, 0:P], rhs=kron_columns[:, 0:K], start=True, stop=True)
         acc.extend([psum_z.tile([P, K], F32, name="z_bank") for i in range(2, Q_TILES)])
         for g in range(PASSES):
             quantise_grad(g, 0)

from contextlib import ExitStack

import concourse.mybir as mybir
from concourse.masks import make_identity

F32 = mybir.dt.float32
BF16 = mybir.dt.bfloat16
U32 = mybir.dt.uint32
U8 = mybir.dt.uint8
E4M3_X4 = mybir.dt.float8_e4m3fn_x4
E5M2_X4 = mybir.dt.float8_e5m2_x4
MULT = mybir.AluOpType.mult
COPY = mybir.ActivationFunctionType.Copy

P = 128
PACK = 4
PAIR = 2
HALVES = PACK // PAIR
K_PASS = P * PACK

ORD, R, B = 3, 8, 1024
Q = 512
K = R**ORD
PASSES = B // K_PASS
Q_TILES = Q // P
CHUNKS = PASSES * HALVES

LAST = PASSES - 1
SCALAR_C = 2
VECTOR_B = 2

WARM_UPS = 2

FLOPS = 2 * Q * K * B
BYTES = ORD * R * B * 2 + Q * B * 2 + Q * K * 4


def tile_fast_tucker_taylor_pa_s_kernel(tc, z, G2, grad_out, out):
    nc = tc.nc
    with ExitStack() as stack:
        consts = stack.enter_context(tc.tile_pool(name="consts", bufs=1))
        factors = stack.enter_context(tc.tile_pool(name="factors", bufs=1))
        per_pass = stack.enter_context(tc.tile_pool(name="per_pass", bufs=PASSES))
        operands = stack.enter_context(tc.tile_pool(name="operands", bufs=1))
        results = stack.enter_context(tc.tile_pool(name="results", bufs=Q_TILES))
        psum_z = stack.enter_context(tc.psum_pool(name="psum_z", bufs=2))
        psum_t = stack.enter_context(tc.psum_pool(name="psum_t", bufs=4))
        psum_acc = stack.enter_context(tc.psum_pool(name="psum_acc", bufs=1))
        stack.enter_context(tc.manual_schedule())

        z_runs = z.rearrange("j r (h w) -> (j r h) w", h=CHUNKS)
        runs_of_two = 2 * R * CHUNKS
        runs_of_one = R * CHUNKS
        z_rows_01 = factors.tile([P, P * PAIR], BF16)
        z_rows_12 = factors.tile([P, P * PAIR], BF16)
        nc.vector.memset(z_rows_01[runs_of_two:P, :], 0.0)
        nc.vector.memset(z_rows_12[0:runs_of_two, :], 0.0)
        nc.sync.dma_start(out=z_rows_01[0:runs_of_two, :], in_=z_runs[0:runs_of_two, :])
        nc.sync.dma_start(out=z_rows_12[runs_of_two:P, :], in_=z_runs[runs_of_one : runs_of_one + runs_of_two, :])

        grad_rows = []
        for half in range(2):
            rows = per_pass.tile([P, 2, B], BF16, name="grad_rows")
            nc.sync.dma_start(
                out=rows[:],
                in_=grad_out[half * 2 * P : (half + 1) * 2 * P, :].rearrange("(j p) n -> p j n", p=P),
            )
            grad_rows.append(rows)

        identity = consts.tile([P, P], F32)
        make_identity(nc, identity[:])

        z_bank_01 = psum_z.tile([P, K], F32, name="z_bank")
        z_cols_01 = z_bank_01[:, 0:P]
        nc.tensor.transpose(z_cols_01, z_rows_01[:].bitcast(F32), identity[:])
        z_bank_12 = psum_z.tile([P, K], F32, name="z_bank")
        z_cols_12 = z_bank_12[:, 0:P]
        nc.tensor.transpose(z_cols_12, z_rows_12[:].bitcast(F32), identity[:])

        acc = [psum_acc.tile([P, K], F32, name="acc%d" % i) for i in range(2)]
        unread = acc[1][:, 0:P]

        def keep_tensor_busy():
            for d in range(WARM_UPS):
                nc.tensor.matmul(unread, lhsT=identity[:], rhs=identity[:], start=True, stop=True)

        keep_tensor_busy()
        z_pairs_01 = z_cols_01.bitcast(BF16).rearrange("p (s r i) -> p s r i", s=4, r=R)
        z_pairs_12 = z_cols_12.bitcast(BF16).rearrange("p (s r i) -> p s r i", s=4, r=R)
        z0_psum = z_pairs_01[:, 0]
        z2_psum = z_pairs_12[:, 3]
        z1_tile = factors.tile([P, R, PASSES * PACK], F32)
        nc.vector.tensor_copy(out=z1_tile[:], in_=z_pairs_01[:, 1])
        z2_tile = factors.tile([P, R, PASSES * PACK], F32)
        nc.scalar.copy(out=z2_tile[:], in_=z_pairs_12[:, 3])
        z1 = z1_tile[:]
        z2 = z2_tile[:]

        pair01 = [per_pass.tile([P, R, R, PACK], F32, name="pair01") for g in range(PASSES)]
        for g in reversed(range(PASSES)):
            t_cols = slice(g * PACK, (g + 1) * PACK)
            nc.vector.tensor_tensor(
                out=pair01[g][:],
                in0=z0_psum[:, :, t_cols].unsqueeze(1).to_broadcast([P, R, R, PACK]),
                in1=z1[:, :, t_cols].unsqueeze(2).to_broadcast([P, R, R, PACK]),
                op=MULT,
            )

        kron = [per_pass.tile([P, R, R * R, PACK], BF16, name="kron", align_bytes=64) for g in range(PASSES)]

        def build_kron(engine, g, c_from, b_from, b_to, z2_view):
            t_cols = slice(g * PACK, (g + 1) * PACK)
            shape = [P, R - c_from, (b_to - b_from) * R, PACK]
            engine.tensor_tensor(
                out=kron[g][:, c_from:, b_from * R : b_to * R],
                in0=pair01[g][:, b_from:b_to].rearrange("p b a t -> p (b a) t").unsqueeze(1).to_broadcast(shape),
                in1=z2_view[:, c_from:, t_cols].unsqueeze(2).to_broadcast(shape),
                op=MULT,
            )

        def build_kron_on_scalar(g, c):
            for t in range(PACK):
                nc.scalar.activation(
                    out=kron[g][:, c, :, t],
                    in_=pair01[g][:, :, :, t].rearrange("p b a -> p (b a)"),
                    func=COPY,
                    scale=z2[:, c, g * PACK + t : g * PACK + t + 1],
                )

        build_kron(nc.gpsimd, LAST, SCALAR_C, VECTOR_B, R, z2)

        grad_grouped = [
            per_pass.tile([P, Q_TILES * P * PACK], BF16, name="grad_grouped", align_bytes=64) for g in range(PASSES)
        ]
        for half in range(2):
            build_kron_on_scalar(LAST, half)
            for g in range(PASSES):
                grouped_words = grad_grouped[g][:].bitcast(F32).rearrange("p (i q u) -> p i q u", i=Q_TILES, u=HALVES)
                bank = psum_t.tile([P, 2, HALVES, P], F32, name="bank")
                for j in range(2):
                    words = grad_rows[half][:, j, :].bitcast(F32)
                    for u in range(HALVES):
                        chunk = g * HALVES + u
                        nc.tensor.transpose(bank[:, j, u, :], words[:, chunk * P : (chunk + 1) * P], identity[:])
                nc.scalar.copy(
                    out=grouped_words[:, 2 * half : 2 * half + 2],
                    in_=bank[:].rearrange("p i u q -> p i q u"),
                )
            keep_tensor_busy()

        kron_codes = operands.tile([P, PASSES, K], U32, align_bytes=64)
        kron_scales = operands.tile([P, PASSES, K], U8, align_bytes=64)
        grad_codes = operands.tile([P, PASSES, Q], U32, align_bytes=64)
        grad_scales = operands.tile([P, PASSES, Q], U8, align_bytes=64)

        def quantise_grad(g, i):
            q_cols = slice(i * P, (i + 1) * P)
            nc.vector.quantize_mx(
                out=grad_codes[:, g, q_cols].bitcast(E5M2_X4),
                scales=grad_scales[:, g, q_cols],
                in_=grad_grouped[g][:, i * P * PACK : (i + 1) * P * PACK],
            )

        def quantise_kron(g):
            nc.vector.quantize_mx(
                out=kron_codes[:, g, :].bitcast(E4M3_X4),
                scales=kron_scales[:, g, :],
                in_=kron[g][:].rearrange("p c w t -> p (c w t)"),
            )

        def multiply(g, i):
            q_cols = slice(i * P, (i + 1) * P)
            nc.tensor.matmul_mx(
                out=acc[i][:],
                lhsT=grad_codes[:, g, q_cols].bitcast(E5M2_X4),
                lhsT_scale=grad_scales[:, g, q_cols],
                rhs=kron_codes[:, g, :].bitcast(E4M3_X4),
                rhs_scale=kron_scales[:, g, :],
                start=(g == 0),
                stop=(g == LAST),
            )

        def store(i, engine_copy, pieces):
            result = results.tile([P, K], F32, name="result")
            width = K // pieces
            for h in range(pieces):
                cols = slice(h * width, (h + 1) * width)
                engine_copy(out=result[:, cols], in_=acc[i][:, cols])
                nc.sync.dma_start(out=out[i * P : (i + 1) * P, cols], in_=result[:, cols])

        build_kron(nc.vector, LAST, SCALAR_C, 0, VECTOR_B, z2_psum)
        build_kron(nc.vector, 0, 0, 0, R, z2_psum)
        kron_columns = kron[0][:].rearrange("p c w t -> p (c w t)")
        nc.tensor.matmul(acc[1][:], lhsT=kron_columns[:, 0:P], rhs=kron_columns[:, 0:K], start=True, stop=True)
        acc.extend([psum_z.tile([P, K], F32, name="z_bank") for i in range(2, Q_TILES)])
        for g in range(PASSES):
            quantise_grad(g, 0)
        for g in range(PASSES):
            quantise_kron(g)
            multiply(g, 0)
        store(0, nc.scalar.copy, 1)
        for i in range(1, Q_TILES):
            for g in range(PASSES):
                quantise_grad(g, i)
                multiply(g, i)
        for i in range(1, Q_TILES):
            store(i, nc.vector.tensor_copy if i == 2 else nc.scalar.copy, 1)
